import numpy as np
import ml_dtypes


def mxq(x, axis, fmt="e4m3"):
    dtype, down = {"e4m3": (ml_dtypes.float8_e4m3fn, 7), "e5m2": (ml_dtypes.float8_e5m2, 14)}[fmt]
    v = np.moveaxis(np.asarray(x, np.float32).astype(ml_dtypes.bfloat16).astype(np.float64), axis, -1)
    blocks = v.reshape(v.shape[:-1] + (-1, 32))
    amax = np.abs(blocks).max(-1, keepdims=True)
    byte = np.maximum(np.where(amax > 0, np.frexp(amax)[1] - 1 + 127, 0) - down, 1)
    scale = np.exp2(byte - 127.0)
    codes = (blocks / scale).astype(np.float32).astype(dtype).astype(np.float64)
    return np.moveaxis((codes * scale).reshape(v.shape), -1, axis)


WIDE = False


def mx_kscale(k):
    if not WIDE:
        return np.ones(k)
    levels = np.array([10, -10, 5, -5, 0])
    a = np.random.permutation(np.resize(levels, k // 512 * 4)).reshape(k // 512, 4)
    idx = np.arange(k)
    return np.exp2(a[idx // 512, idx % 128 // 32])


BF16 = ml_dtypes.bfloat16


def bf(x):
    return np.asarray(x, np.float32).astype(BF16)


def f64(x):
    return np.asarray(x).astype(np.float64)


B, T, C, KW = 2, 1024, 512, 3
PAD = KW // 2


def setup_inputs():
    s = mx_kscale(C)
    return {"x": bf(np.random.standard_normal((B, T, C)) * s),
            "w1": bf(np.random.standard_normal((C, C)) / np.sqrt(C) / s[None, :]),
            "b1": bf(np.random.standard_normal(C) * 0.2),
            "w2": bf(np.random.standard_normal((C, KW)) * 0.8),
            "b2": bf(np.random.standard_normal(C) * 0.2)}


def reference(x, w1, b1, w2, b2):
    h = (mxq(f64(x), 2, "e4m3") @ mxq(f64(w1), 1, "e4m3").T) + f64(b1)
    hp = np.pad(h, ((0, 0), (PAD, PAD), (0, 0)))
    taps = f64(w2)
    y = hp[:, 0:T, :] * taps[:, 0]
    for j in range(1, KW):
        y = y + hp[:, j:j + T, :] * taps[:, j]
    return y + f64(b2)

@@ -1,0 +1,180 @@
+from concourse import mybir
+from concourse.masks import make_identity
+
+F32 = mybir.dt.float32
+BF16 = mybir.dt.bfloat16
+U32 = mybir.dt.uint32
+U8 = mybir.dt.uint8
+FP8X4 = mybir.dt.float8_e4m3fn_x4
+MULT = mybir.AluOpType.mult
+ADD = mybir.AluOpType.add
+SUBTRACT = mybir.AluOpType.subtract
+IDENTITY = mybir.ActivationFunctionType.Identity
+
+B, T, C, KW = 2, 1024, 512, 3
+P = 128
+PACK = 4
+HALVES = 2
+WORDS = C // 2
+CHUNK = 512
+ROW_BLOCKS = CHUNK // P
+D_BLOCKS = C // P
+CHUNKS = T // CHUNK
+
+FLOPS = 2 * B * T * C * C + 2 * KW * B * T * C
+
+
+def tile_cvim_pa_kernel(tc, x, w1, b1, w2, b2, out):
+    nc = tc.nc
+
+    with (
+        tc.tile_pool(name="keep", bufs=1) as keep,
+        tc.tile_pool(name="stage", bufs=2) as stage,
+        tc.tile_pool(name="leave", bufs=4) as leave,
+        tc.psum_pool(name="turned", bufs=2) as turned,
+        tc.psum_pool(name="sums", bufs=4) as sums,
+        tc.psum_pool(name="back", bufs=2) as back,
+    ):
+        taps_bf = keep.tile([P, D_BLOCKS, KW], BF16)
+        b1_bf = keep.tile([P, D_BLOCKS], BF16)
+        b2_bf = keep.tile([P, D_BLOCKS], BF16)
+        with nc.allow_non_contiguous_dma(reason="one value of a 512-long vector to a partition"):
+            nc.scalar.dma_start(out=taps_bf[:], in_=w2.rearrange("(m p) j -> p m j", p=P))
+            nc.scalar.dma_start(out=b1_bf[:], in_=b1.rearrange("(m p) -> p m", p=P))
+            nc.scalar.dma_start(out=b2_bf[:], in_=b2.rearrange("(m p) -> p m", p=P))
+
+        w_rows = keep.tile([P, ROW_BLOCKS * C], BF16)
+        nc.sync.dma_start(
+            out=w_rows[:].rearrange("p (r c) -> p r c", c=C),
+            in_=w1.rearrange("(r p) c -> p r c", p=P),
+        )
+        x_rows = {}
+        for b in range(B):
+            for n in range(CHUNKS):
+                x_rows[b, n] = keep.tile([P, ROW_BLOCKS * C], BF16, name="x_rows_%d_%d" % (b, n))
+                nc.sync.dma_start(
+                    out=x_rows[b, n][:].rearrange("p (r c) -> p r c", c=C),
+                    in_=x[b, n * CHUNK : (n + 1) * CHUNK, :].rearrange("(r p) c -> p r c", p=P),
+                )
+
+        ident = keep.tile([P, P], F32)
+        make_identity(nc, ident[:])
+
+        def quantise_rows(rows, codes, scales, copy_out):
+            words = rows[:].bitcast(F32)
+            grouped = stage.tile([P, CHUNK * PACK], BF16, align_bytes=64)
+            grouped_words = grouped[:].bitcast(F32).rearrange("p (t u) -> p t u", u=HALVES)
+            for pair in range(ROW_BLOCKS // 2):
+                flipped = turned.tile([P, HALVES, 2 * P], F32)
+                for r in (2 * pair, 2 * pair + 1):
+                    for u in range(HALVES):
+                        nc.tensor.transpose(
+                            flipped[:, u, (r % 2) * P : (r % 2 + 1) * P],
+                            words[:, r * WORDS + u * P : r * WORDS + (u + 1) * P],
+                            ident[:],
+                        )
+                copy_out(
+                    out=grouped_words[:, 2 * pair * P : (2 * pair + 2) * P, :],
+                    in_=flipped[:].rearrange("p u t -> p t u"),
+                )
+            nc.vector.quantize_mx(out=codes.bitcast(FP8X4), scales=scales, in_=grouped[:])
+
+        w_codes = keep.tile([P, C], U32, align_bytes=64)
+        w_scales = keep.tile([P, C], U8, align_bytes=64)
+        quantise_rows(w_rows, w_codes[:], w_scales[:], nc.vector.tensor_copy)
+
+        x_codes = keep.tile([P, B, CHUNKS, CHUNK], U32, align_bytes=64)
+        x_scales = keep.tile([P, B, CHUNKS, CHUNK], U8, align_bytes=64)
+
+        def quantise_chunk(b, n):
+            quantise_rows(x_rows[b, n], x_codes[:, b, n, :], x_scales[:, b, n, :], nc.scalar.copy)
+
+        taps = keep.tile([P, D_BLOCKS, KW], F32)
+        nc.vector.tensor_copy(out=taps[:], in_=taps_bf[:])
+        tap_bias = keep.tile([P, D_BLOCKS, KW], F32)
+        nc.vector.tensor_tensor(
+            out=tap_bias[:],
+            in0=taps[:],
+            in1=b1_bf[:].unsqueeze(2).to_broadcast([P, D_BLOCKS, KW]),
+            op=MULT,
+        )
+        inner_bias = keep.tile([P, D_BLOCKS], F32)
+        nc.vector.tensor_reduce(out=inner_bias[:], in_=tap_bias[:], axis=mybir.AxisListType.X, op=ADD)
+        nc.vector.tensor_tensor(out=inner_bias[:], in0=inner_bias[:], in1=b2_bf[:], op=ADD)
+        first_bias = keep.tile([P, D_BLOCKS], F32)
+        nc.vector.tensor_tensor(out=first_bias[:], in0=inner_bias[:], in1=tap_bias[:, :, 0], op=SUBTRACT)
+
+        y_cols = {}
+        for b in range(B):
+            y_cols[b] = keep.tile([P, D_BLOCKS, T], F32, name="y_cols_%d" % b)
+
+        def convolve_chunk(b, n):
+            t0 = n * CHUNK
+            y = y_cols[b]
+            acc = {}
+            for m in range(D_BLOCKS):
+                acc[m] = sums.tile([P, CHUNK], F32, name="acc")
+                nc.tensor.matmul_mx(
+                    out=acc[m][:],
+                    lhsT=w_codes[:, m * P : (m + 1) * P].bitcast(FP8X4),
+                    lhsT_scale=w_scales[:, m * P : (m + 1) * P],
+                    rhs=x_codes[:, b, n, :].bitcast(FP8X4),
+                    rhs_scale=x_scales[:, b, n, :],
+                    start=True,
+                    stop=True,
+                )
+            if n == 0:
+                nc.scalar.copy(out=y[:, :, 0:1], in_=first_bias[:].unsqueeze(2))
+            n_left = min(CHUNK, T - 1 - t0)
+            for m in range(D_BLOCKS):
+                nc.scalar.activation(
+                    out=y[:, m, t0 + 1 : t0 + 1 + n_left],
+                    in_=acc[m][:, 0:n_left],
+                    func=IDENTITY,
+                    scale=taps[:, m, 0:1],
+                    bias=inner_bias[:, m : m + 1],
+                )
+            for m in range(D_BLOCKS):
+                nc.vector.scalar_tensor_tensor(
+                    out=y[:, m, t0 : t0 + CHUNK],
+                    in0=acc[m][:],
+                    scalar=taps[:, m, 1:2],
+                    in1=y[:, m, t0 : t0 + CHUNK],
+                    op0=MULT,
+                    op1=ADD,
+                )
+            skip = 1 if n == 0 else 0
+            for m in range(D_BLOCKS):
+                nc.vector.scalar_tensor_tensor(
+                    out=y[:, m, t0 - 1 + skip : t0 + CHUNK - 1],
+                    in0=acc[m][:, skip:CHUNK],
+                    scalar=taps[:, m, 2:3],
+                    in1=y[:, m, t0 - 1 + skip : t0 + CHUNK - 1],
+                    op0=MULT,
+                    op1=ADD,
+                )
+            if n == CHUNKS - 1:
+                nc.vector.tensor_tensor(
+                    out=y[:, :, T - 1 : T], in0=y[:, :, T - 1 : T], in1=tap_bias[:, :, 2:3], op=SUBTRACT
+                )
+
+        def store_block(b, k):
+            y_rows_ps = back.tile([P, C], F32)
+            for m in range(D_BLOCKS):
+                nc.tensor.transpose(
+                    y_rows_ps[:, m * P : (m + 1) * P], y_cols[b][:, m, k * P : (k + 1) * P], ident[:]
+                )
+            y_rows = leave.tile([P, C], F32)
+            nc.scalar.copy(out=y_rows[:], in_=y_rows_ps[:])
+            nc.sync.dma_start(out=out[b, k * P : (k + 1) * P, :], in_=y_rows[:])
+
+        order = [(b, n) for b in range(B) for n in range(CHUNKS)]
+        quantise_chunk(*order[0])
+        for i, (b, n) in enumerate(order):
+            if i + 1 < len(order):
+                quantise_chunk(*order[i + 1])
+            convolve_chunk(b, n)
+            first = max(n * ROW_BLOCKS - 1, 0)
+            last = (n + 1) * ROW_BLOCKS - 1 if n + 1 < CHUNKS else (n + 1) * ROW_BLOCKS
+            for k in range(first, last):
+                store_block(b, k)

@@ -29,11 +29,11 @@ def tile_cvim_pa_kernel(tc, x, w1, b1, w2, b2, out):
 
     with (
         tc.tile_pool(name="keep", bufs=1) as keep,
-        tc.tile_pool(name="stage", bufs=2) as stage,
-        tc.tile_pool(name="leave", bufs=4) as leave,
-        tc.psum_pool(name="turned", bufs=2) as turned,
-        tc.psum_pool(name="sums", bufs=4) as sums,
-        tc.psum_pool(name="back", bufs=2) as back,
+        tc.tile_pool(name="stage", bufs=3) as stage,
+        tc.tile_pool(name="work", bufs=4) as work,
+        tc.tile_pool(name="leave", bufs=8) as leave,
+        tc.psum_pool(name="psum", bufs=8) as psum,
+        tc.manual_schedule(),
     ):
         taps_bf = keep.tile([P, D_BLOCKS, KW], BF16)
         b1_bf = keep.tile([P, D_BLOCKS], BF16)
@@ -60,12 +60,26 @@ def tile_cvim_pa_kernel(tc, x, w1, b1, w2, b2, out):
         ident = keep.tile([P, P], F32)
         make_identity(nc, ident[:])
 
-        def quantise_rows(rows, codes, scales, copy_out):
+        taps = keep.tile([P, D_BLOCKS, KW], F32)
+        nc.vector.tensor_copy(out=taps[:], in_=taps_bf[:])
+        tap_bias = keep.tile([P, D_BLOCKS, KW], F32)
+        nc.vector.tensor_tensor(
+            out=tap_bias[:],
+            in0=taps[:],
+            in1=b1_bf[:].unsqueeze(2).to_broadcast([P, D_BLOCKS, KW]),
+            op=MULT,
+        )
+        tap_bias_sum = keep.tile([P, D_BLOCKS], F32)
+        nc.vector.tensor_reduce(out=tap_bias_sum[:], in_=tap_bias[:], axis=mybir.AxisListType.X, op=ADD)
+        inner_bias = keep.tile([P, D_BLOCKS], F32)
+        nc.vector.tensor_tensor(out=inner_bias[:], in0=tap_bias_sum[:], in1=b2_bf[:], op=ADD)
+
+        def quantise_rows(rows, codes, scales):
             words = rows[:].bitcast(F32)
             grouped = stage.tile([P, CHUNK * PACK], BF16, align_bytes=64)
             grouped_words = grouped[:].bitcast(F32).rearrange("p (t u) -> p t u", u=HALVES)
-            for pair in range(ROW_BLOCKS // 2):
-                flipped = turned.tile([P, HALVES, 2 * P], F32)
+            for pair, copy_out in enumerate((nc.scalar.copy, nc.vector.tensor_copy)):
+                flipped = psum.tile([P, HALVES, 2 * P], F32, tag="bank")
                 for r in (2 * pair, 2 * pair + 1):
                     for u in range(HALVES):
                         nc.tensor.transpose(
@@ -81,41 +95,22 @@ def tile_cvim_pa_kernel(tc, x, w1, b1, w2, b2, out):
 
         w_codes = keep.tile([P, C], U32, align_bytes=64)
         w_scales = keep.tile([P, C], U8, align_bytes=64)
-        quantise_rows(w_rows, w_codes[:], w_scales[:], nc.vector.tensor_copy)
-
         x_codes = keep.tile([P, B, CHUNKS, CHUNK], U32, align_bytes=64)
         x_scales = keep.tile([P, B, CHUNKS, CHUNK], U8, align_bytes=64)
-
-        def quantise_chunk(b, n):
-            quantise_rows(x_rows[b, n], x_codes[:, b, n, :], x_scales[:, b, n, :], nc.scalar.copy)
-
-        taps = keep.tile([P, D_BLOCKS, KW], F32)
-        nc.vector.tensor_copy(out=taps[:], in_=taps_bf[:])
-        tap_bias = keep.tile([P, D_BLOCKS, KW], F32)
-        nc.vector.tensor_tensor(
-            out=tap_bias[:],
-            in0=taps[:],
-            in1=b1_bf[:].unsqueeze(2).to_broadcast([P, D_BLOCKS, KW]),
-            op=MULT,
-        )
-        inner_bias = keep.tile([P, D_BLOCKS], F32)
-        nc.vector.tensor_reduce(out=inner_bias[:], in_=tap_bias[:], axis=mybir.AxisListType.X, op=ADD)
-        nc.vector.tensor_tensor(out=inner_bias[:], in0=inner_bias[:], in1=b2_bf[:], op=ADD)
-        first_bias = keep.tile([P, D_BLOCKS], F32)
-        nc.vector.tensor_tensor(out=first_bias[:], in0=inner_bias[:], in1=tap_bias[:, :, 0], op=SUBTRACT)
-
-        y_cols = {}
+        quantise_rows(w_rows, w_codes[:], w_scales[:])
         for b in range(B):
-            y_cols[b] = keep.tile([P, D_BLOCKS, T], F32, name="y_cols_%d" % b)
+            for n in range(CHUNKS):
+                quantise_rows(x_rows[b, n], x_codes[:, b, n, :], x_scales[:, b, n, :])
 
-        def convolve_chunk(b, n):
-            t0 = n * CHUNK
-            y = y_cols[b]
-            acc = {}
-            for m in range(D_BLOCKS):
-                acc[m] = sums.tile([P, CHUNK], F32, name="acc")
+        acc = {}
+        y_cols = {}
+
+        def middle_tap(b, m):
+            y_cols[b, m] = work.tile([P, T], F32, name="y_cols")
+            for n in range(CHUNKS):
+                acc[b, m, n] = psum.tile([P, CHUNK], F32, name="acc", tag="bank")
                 nc.tensor.matmul_mx(
-                    out=acc[m][:],
+                    out=acc[b, m, n][:],
                     lhsT=w_codes[:, m * P : (m + 1) * P].bitcast(FP8X4),
                     lhsT_scale=w_scales[:, m * P : (m + 1) * P],
                     rhs=x_codes[:, b, n, :].bitcast(FP8X4),
@@ -123,58 +118,67 @@ def tile_cvim_pa_kernel(tc, x, w1, b1, w2, b2, out):
                     start=True,
                     stop=True,
                 )
-            if n == 0:
-                nc.scalar.copy(out=y[:, :, 0:1], in_=first_bias[:].unsqueeze(2))
-            n_left = min(CHUNK, T - 1 - t0)
-            for m in range(D_BLOCKS):
+            for n in range(CHUNKS):
                 nc.scalar.activation(
-                    out=y[:, m, t0 + 1 : t0 + 1 + n_left],
-                    in_=acc[m][:, 0:n_left],
+                    out=y_cols[b, m][:, n * CHUNK : (n + 1) * CHUNK],
+                    in_=acc[b, m, n][:],
                     func=IDENTITY,
-                    scale=taps[:, m, 0:1],
+                    scale=taps[:, m, 1:2],
                     bias=inner_bias[:, m : m + 1],
                 )
-            for m in range(D_BLOCKS):
+
+        def side_taps(b, m):
+            y = y_cols[b, m]
+            for n in range(CHUNKS):
+                t0 = n * CHUNK
+                skip = 1 if n == 0 else 0
                 nc.vector.scalar_tensor_tensor(
-                    out=y[:, m, t0 : t0 + CHUNK],
-                    in0=acc[m][:],
-                    scalar=taps[:, m, 1:2],
-                    in1=y[:, m, t0 : t0 + CHUNK],
-                    op0=MULT,
-                    op1=ADD,
-                )
-            skip = 1 if n == 0 else 0
-            for m in range(D_BLOCKS):
-                nc.vector.scalar_tensor_tensor(
-                    out=y[:, m, t0 - 1 + skip : t0 + CHUNK - 1],
-                    in0=acc[m][:, skip:CHUNK],
+                    out=y[:, t0 - 1 + skip : t0 + CHUNK - 1],
+                    in0=acc[b, m, n][:, skip:CHUNK],
                     scalar=taps[:, m, 2:3],
-                    in1=y[:, m, t0 - 1 + skip : t0 + CHUNK - 1],
+                    in1=y[:, t0 - 1 + skip : t0 + CHUNK - 1],
                     op0=MULT,
                     op1=ADD,
                 )
-            if n == CHUNKS - 1:
-                nc.vector.tensor_tensor(
-                    out=y[:, :, T - 1 : T], in0=y[:, :, T - 1 : T], in1=tap_bias[:, :, 2:3], op=SUBTRACT
+            nc.vector.tensor_tensor(
+                out=y[:, 0 : T : T - 1],
+                in0=y[:, 0 : T : T - 1],
+                in1=tap_bias[:, m, 0 : KW : KW - 1],
+                op=SUBTRACT,
+            )
+            for n in range(CHUNKS):
+                t0 = n * CHUNK
+                width = min(CHUNK, T - 1 - t0)
+                nc.vector.scalar_tensor_tensor(
+                    out=y[:, t0 + 1 : t0 + 1 + width],
+                    in0=acc[b, m, n][:, 0:width],
+                    scalar=taps[:, m, 0:1],
+                    in1=y[:, t0 + 1 : t0 + 1 + width],
+                    op0=MULT,
+                    op1=ADD,
                 )
 
-        def store_block(b, k):
-            y_rows_ps = back.tile([P, C], F32)
-            for m in range(D_BLOCKS):
-                nc.tensor.transpose(
-                    y_rows_ps[:, m * P : (m + 1) * P], y_cols[b][:, m, k * P : (k + 1) * P], ident[:]
+        def store_unit(b, m):
+            for n in range(CHUNKS):
+                y_rows_ps = psum.tile([P, ROW_BLOCKS, P], F32, tag="bank")
+                for k in range(ROW_BLOCKS):
+                    t0 = n * CHUNK + k * P
+                    nc.tensor.transpose(y_rows_ps[:, k, :], y_cols[b, m][:, t0 : t0 + P], ident[:])
+                y_rows = leave.tile([P, ROW_BLOCKS, P], F32)
+                nc.scalar.copy(out=y_rows[:], in_=y_rows_ps[:])
+                nc.sync.dma_start(
+                    out=out[b, n * CHUNK : (n + 1) * CHUNK, m * P : (m + 1) * P].rearrange(
+                        "(k p) d -> p k d", p=P
+                    ),
+                    in_=y_rows[:],
                 )
-            y_rows = leave.tile([P, C], F32)
-            nc.scalar.copy(out=y_rows[:], in_=y_rows_ps[:])
-            nc.sync.dma_start(out=out[b, k * P : (k + 1) * P, :], in_=y_rows[:])
 
-        order = [(b, n) for b in range(B) for n in range(CHUNKS)]
-        quantise_chunk(*order[0])
-        for i, (b, n) in enumerate(order):
-            if i + 1 < len(order):
-                quantise_chunk(*order[i + 1])
-            convolve_chunk(b, n)
-            first = max(n * ROW_BLOCKS - 1, 0)
-            last = (n + 1) * ROW_BLOCKS - 1 if n + 1 < CHUNKS else (n + 1) * ROW_BLOCKS
-            for k in range(first, last):
-                store_block(b, k)
+        units = [(b, m) for b in range(B) for m in range(D_BLOCKS)]
+        middle_tap(*units[0])
+        for i, unit in enumerate(units):
+            if i + 1 < len(units):
+                middle_tap(*units[i + 1])
+            side_taps(*unit)
+            if i > 0:
+                store_unit(*units[i - 1])
+        store_unit(*units[-1])

@@ -43,36 +43,37 @@ def tile_cvim_pa_kernel(tc, x, w1, b1, w2, b2, out):
             nc.scalar.dma_start(out=b1_bf[:], in_=b1.rearrange("(m p) -> p m", p=P))
             nc.scalar.dma_start(out=b2_bf[:], in_=b2.rearrange("(m p) -> p m", p=P))
 
-        w_rows = keep.tile([P, ROW_BLOCKS * C], BF16)
-        nc.sync.dma_start(
-            out=w_rows[:].rearrange("p (r c) -> p r c", c=C),
-            in_=w1.rearrange("(r p) c -> p r c", p=P),
-        )
+        def load_rows(rows_dram, name):
+            rows = keep.tile([P, ROW_BLOCKS * C], BF16, name=name)
+            for pair in range(ROW_BLOCKS // 2):
+                nc.sync.dma_start(
+                    out=rows[:, 2 * pair * C : (2 * pair + 2) * C].rearrange("p (r c) -> p r c", c=C),
+                    in_=rows_dram[2 * pair * P : (2 * pair + 2) * P, :].rearrange("(r p) c -> p r c", p=P),
+                )
+            return rows
+
+        w_rows = load_rows(w1, "w_rows")
         x_rows = {}
         for b in range(B):
             for n in range(CHUNKS):
-                x_rows[b, n] = keep.tile([P, ROW_BLOCKS * C], BF16, name="x_rows_%d_%d" % (b, n))
-                nc.sync.dma_start(
-                    out=x_rows[b, n][:].rearrange("p (r c) -> p r c", c=C),
-                    in_=x[b, n * CHUNK : (n + 1) * CHUNK, :].rearrange("(r p) c -> p r c", p=P),
-                )
+                x_rows[b, n] = load_rows(x[b, n * CHUNK : (n + 1) * CHUNK, :], "x_rows_%d_%d" % (b, n))
 
         ident = keep.tile([P, P], F32)
         make_identity(nc, ident[:])
 
         taps = keep.tile([P, D_BLOCKS, KW], F32)
-        nc.vector.tensor_copy(out=taps[:], in_=taps_bf[:])
+        nc.gpsimd.tensor_copy(out=taps[:], in_=taps_bf[:])
         tap_bias = keep.tile([P, D_BLOCKS, KW], F32)
-        nc.vector.tensor_tensor(
+        nc.gpsimd.tensor_tensor(
             out=tap_bias[:],
             in0=taps[:],
             in1=b1_bf[:].unsqueeze(2).to_broadcast([P, D_BLOCKS, KW]),
             op=MULT,
         )
-        tap_bias_sum = keep.tile([P, D_BLOCKS], F32)
-        nc.vector.tensor_reduce(out=tap_bias_sum[:], in_=tap_bias[:], axis=mybir.AxisListType.X, op=ADD)
         inner_bias = keep.tile([P, D_BLOCKS], F32)
-        nc.vector.tensor_tensor(out=inner_bias[:], in0=tap_bias_sum[:], in1=b2_bf[:], op=ADD)
+        nc.gpsimd.tensor_tensor(out=inner_bias[:], in0=tap_bias[:, :, 0], in1=b2_bf[:], op=ADD)
+        for j in range(1, KW):
+            nc.gpsimd.tensor_tensor(out=inner_bias[:], in0=inner_bias[:], in1=tap_bias[:, :, j], op=ADD)
 
         def quantise_rows(rows, codes, scales):
             words = rows[:].bitcast(F32)
@@ -106,7 +107,8 @@ def tile_cvim_pa_kernel(tc, x, w1, b1, w2, b2, out):
         y_cols = {}
 
         def middle_tap(b, m):
-            y_cols[b, m] = work.tile([P, T], F32, name="y_cols")
+            y = work.tile([P, T], F32, name="y_cols")
+            y_cols[b, m] = y
             for n in range(CHUNKS):
                 acc[b, m, n] = psum.tile([P, CHUNK], F32, name="acc", tag="bank")
                 nc.tensor.matmul_mx(
@@ -120,12 +122,18 @@ def tile_cvim_pa_kernel(tc, x, w1, b1, w2, b2, out):
                 )
             for n in range(CHUNKS):
                 nc.scalar.activation(
-                    out=y_cols[b, m][:, n * CHUNK : (n + 1) * CHUNK],
+                    out=y[:, n * CHUNK : (n + 1) * CHUNK],
                     in_=acc[b, m, n][:],
                     func=IDENTITY,
                     scale=taps[:, m, 1:2],
                     bias=inner_bias[:, m : m + 1],
                 )
+            nc.gpsimd.tensor_tensor(
+                out=y[:, 0 : T : T - 1],
+                in0=y[:, 0 : T : T - 1],
+                in1=tap_bias[:, m, 0 : KW : KW - 1],
+                op=SUBTRACT,
+            )
 
         def side_taps(b, m):
             y = y_cols[b, m]
@@ -140,12 +148,6 @@ def tile_cvim_pa_kernel(tc, x, w1, b1, w2, b2, out):
                     op0=MULT,
                     op1=ADD,
                 )
-            nc.vector.tensor_tensor(
-                out=y[:, 0 : T : T - 1],
-                in0=y[:, 0 : T : T - 1],
-                in1=tap_bias[:, m, 0 : KW : KW - 1],
-                op=SUBTRACT,
-            )
             for n in range(CHUNKS):
                 t0 = n * CHUNK
                 width = min(CHUNK, T - 1 - t0)

@@ -20,6 +20,7 @@ CHUNK = 512
 ROW_BLOCKS = CHUNK // P
 D_BLOCKS = C // P
 CHUNKS = T // CHUNK
+AHEAD = 2
 
 FLOPS = 2 * B * T * C * C + 2 * KW * B * T * C
 
@@ -30,9 +31,10 @@ def tile_cvim_pa_kernel(tc, x, w1, b1, w2, b2, out):
     with (
         tc.tile_pool(name="keep", bufs=1) as keep,
         tc.tile_pool(name="stage", bufs=3) as stage,
-        tc.tile_pool(name="work", bufs=4) as work,
+        tc.tile_pool(name="work", bufs=AHEAD + 3) as work,
         tc.tile_pool(name="leave", bufs=8) as leave,
-        tc.psum_pool(name="psum", bufs=8) as psum,
+        tc.psum_pool(name="psum", bufs=(AHEAD + 1) * CHUNKS) as psum,
+        tc.psum_pool(name="psum_back", bufs=2) as psum_back,
         tc.manual_schedule(),
     ):
         taps_bf = keep.tile([P, D_BLOCKS, KW], BF16)
@@ -162,7 +164,7 @@ def tile_cvim_pa_kernel(tc, x, w1, b1, w2, b2, out):
 
         def store_unit(b, m):
             for n in range(CHUNKS):
-                y_rows_ps = psum.tile([P, ROW_BLOCKS, P], F32, tag="bank")
+                y_rows_ps = psum_back.tile([P, ROW_BLOCKS, P], F32)
                 for k in range(ROW_BLOCKS):
                     t0 = n * CHUNK + k * P
                     nc.tensor.transpose(y_rows_ps[:, k, :], y_cols[b, m][:, t0 : t0 + P], ident[:])
@@ -176,10 +178,11 @@ def tile_cvim_pa_kernel(tc, x, w1, b1, w2, b2, out):
                 )
 
         units = [(b, m) for b in range(B) for m in range(D_BLOCKS)]
-        middle_tap(*units[0])
+        for unit in units[:AHEAD]:
+            middle_tap(*unit)
         for i, unit in enumerate(units):
-            if i + 1 < len(units):
-                middle_tap(*units[i + 1])
+            if i + AHEAD < len(units):
+                middle_tap(*units[i + AHEAD])
             side_taps(*unit)
             if i > 0:
                 store_unit(*units[i - 1])

@@ -77,7 +77,7 @@ def tile_cvim_pa_kernel(tc, x, w1, b1, w2, b2, out):
         for j in range(1, KW):
             nc.gpsimd.tensor_tensor(out=inner_bias[:], in0=inner_bias[:], in1=tap_bias[:, :, j], op=ADD)
 
-        def quantise_rows(rows, codes, scales):
+        def regroup_rows(rows):
             words = rows[:].bitcast(F32)
             grouped = stage.tile([P, CHUNK * PACK], BF16, align_bytes=64)
             grouped_words = grouped[:].bitcast(F32).rearrange("p (t u) -> p t u", u=HALVES)
@@ -94,16 +94,27 @@ def tile_cvim_pa_kernel(tc, x, w1, b1, w2, b2, out):
                     out=grouped_words[:, 2 * pair * P : (2 * pair + 2) * P, :],
                     in_=flipped[:].rearrange("p u t -> p t u"),
                 )
-            nc.vector.quantize_mx(out=codes.bitcast(FP8X4), scales=scales, in_=grouped[:])
+            return grouped
 
         w_codes = keep.tile([P, C], U32, align_bytes=64)
         w_scales = keep.tile([P, C], U8, align_bytes=64)
         x_codes = keep.tile([P, B, CHUNKS, CHUNK], U32, align_bytes=64)
         x_scales = keep.tile([P, B, CHUNKS, CHUNK], U8, align_bytes=64)
-        quantise_rows(w_rows, w_codes[:], w_scales[:])
+        sources = [(w_rows, w_codes[:], w_scales[:])]
         for b in range(B):
             for n in range(CHUNKS):
-                quantise_rows(x_rows[b, n], x_codes[:, b, n, :], x_scales[:, b, n, :])
+                sources.append((x_rows[b, n], x_codes[:, b, n, :], x_scales[:, b, n, :]))
+        grouped_tiles = []
+
+        def quantise(k):
+            rows, codes, scales = sources[k]
+            nc.vector.quantize_mx(out=codes.bitcast(FP8X4), scales=scales, in_=grouped_tiles[k][:])
+
+        for k, (rows, codes, scales) in enumerate(sources):
+            grouped_tiles.append(regroup_rows(rows))
+            if k > 0:
+                quantise(k - 1)
+        quantise(len(sources) - 1)
 
         acc = {}
         y_cols = {}
@@ -137,30 +148,31 @@ def tile_cvim_pa_kernel(tc, x, w1, b1, w2, b2, out):
                 op=SUBTRACT,
             )
 
-        def side_taps(b, m):
+        def right_tap(b, m, n):
             y = y_cols[b, m]
-            for n in range(CHUNKS):
-                t0 = n * CHUNK
-                skip = 1 if n == 0 else 0
-                nc.vector.scalar_tensor_tensor(
-                    out=y[:, t0 - 1 + skip : t0 + CHUNK - 1],
-                    in0=acc[b, m, n][:, skip:CHUNK],
-                    scalar=taps[:, m, 2:3],
-                    in1=y[:, t0 - 1 + skip : t0 + CHUNK - 1],
-                    op0=MULT,
-                    op1=ADD,
-                )
-            for n in range(CHUNKS):
-                t0 = n * CHUNK
-                width = min(CHUNK, T - 1 - t0)
-                nc.vector.scalar_tensor_tensor(
-                    out=y[:, t0 + 1 : t0 + 1 + width],
-                    in0=acc[b, m, n][:, 0:width],
-                    scalar=taps[:, m, 0:1],
-                    in1=y[:, t0 + 1 : t0 + 1 + width],
-                    op0=MULT,
-                    op1=ADD,
-                )
+            t0 = n * CHUNK
+            skip = 1 if n == 0 else 0
+            nc.vector.scalar_tensor_tensor(
+                out=y[:, t0 - 1 + skip : t0 + CHUNK - 1],
+                in0=acc[b, m, n][:, skip:CHUNK],
+                scalar=taps[:, m, 2:3],
+                in1=y[:, t0 - 1 + skip : t0 + CHUNK - 1],
+                op0=MULT,
+                op1=ADD,
+            )
+
+        def left_tap(b, m, n):
+            y = y_cols[b, m]
+            t0 = n * CHUNK
+            width = min(CHUNK, T - 1 - t0)
+            nc.vector.scalar_tensor_tensor(
+                out=y[:, t0 + 1 : t0 + 1 + width],
+                in0=acc[b, m, n][:, 0:width],
+                scalar=taps[:, m, 0:1],
+                in1=y[:, t0 + 1 : t0 + 1 + width],
+                op0=MULT,
+                op1=ADD,
+            )
 
         def store_unit(b, m):
             for n in range(CHUNKS):
@@ -180,10 +192,16 @@ def tile_cvim_pa_kernel(tc, x, w1, b1, w2, b2, out):
         units = [(b, m) for b in range(B) for m in range(D_BLOCKS)]
         for unit in units[:AHEAD]:
             middle_tap(*unit)
+        right_tap(*units[0], 0)
         for i, unit in enumerate(units):
             if i + AHEAD < len(units):
                 middle_tap(*units[i + AHEAD])
-            side_taps(*unit)
+            for n in range(1, CHUNKS):
+                right_tap(*unit, n)
+            if i + 1 < len(units):
+                right_tap(*units[i + 1], 0)
+            for n in range(CHUNKS):
+                left_tap(*unit, n)
             if i > 0:
                 store_unit(*units[i - 1])
         store_unit(*units[-1])

@@ -21,6 +21,7 @@ ROW_BLOCKS = CHUNK // P
 D_BLOCKS = C // P
 CHUNKS = T // CHUNK
 AHEAD = 2
+WARM = 5
 
 FLOPS = 2 * B * T * C * C + 2 * KW * B * T * C
 
@@ -37,6 +38,12 @@ def tile_cvim_pa_kernel(tc, x, w1, b1, w2, b2, out):
         tc.psum_pool(name="psum_back", bufs=2) as psum_back,
         tc.manual_schedule(),
     ):
+        zeros = keep.tile([P, CHUNK], BF16)
+        nc.vector.memset(zeros[:], 0.0)
+        unread = psum.tile([P, CHUNK], F32, tag="bank")
+        for k in range(WARM):
+            nc.tensor.matmul(out=unread[:], lhsT=zeros[:, 0:P], rhs=zeros[:], start=True, stop=True)
+
         taps_bf = keep.tile([P, D_BLOCKS, KW], BF16)
         b1_bf = keep.tile([P, D_BLOCKS], BF16)
         b2_bf = keep.tile([P, D_BLOCKS], BF16)
@@ -81,7 +88,7 @@ def tile_cvim_pa_kernel(tc, x, w1, b1, w2, b2, out):
             words = rows[:].bitcast(F32)
             grouped = stage.tile([P, CHUNK * PACK], BF16, align_bytes=64)
             grouped_words = grouped[:].bitcast(F32).rearrange("p (t u) -> p t u", u=HALVES)
-            for pair, copy_out in enumerate((nc.scalar.copy, nc.vector.tensor_copy)):
+            for pair in range(ROW_BLOCKS // 2):
                 flipped = psum.tile([P, HALVES, 2 * P], F32, tag="bank")
                 for r in (2 * pair, 2 * pair + 1):
                     for u in range(HALVES):
@@ -90,7 +97,7 @@ def tile_cvim_pa_kernel(tc, x, w1, b1, w2, b2, out):
                             words[:, r * WORDS + u * P : r * WORDS + (u + 1) * P],
                             ident[:],
                         )
-                copy_out(
+                nc.scalar.copy(
                     out=grouped_words[:, 2 * pair * P : (2 * pair + 2) * P, :],
                     in_=flipped[:].rearrange("p u t -> p t u"),
                 )
@@ -110,11 +117,9 @@ def tile_cvim_pa_kernel(tc, x, w1, b1, w2, b2, out):
             rows, codes, scales = sources[k]
             nc.vector.quantize_mx(out=codes.bitcast(FP8X4), scales=scales, in_=grouped_tiles[k][:])
 
-        for k, (rows, codes, scales) in enumerate(sources):
-            grouped_tiles.append(regroup_rows(rows))
-            if k > 0:
-                quantise(k - 1)
-        quantise(len(sources) - 1)
+        for k in range(len(sources) - 1):
+            grouped_tiles.append(regroup_rows(sources[k][0]))
+            quantise(k)
 
         acc = {}
         y_cols = {}
@@ -192,6 +197,7 @@ def tile_cvim_pa_kernel(tc, x, w1, b1, w2, b2, out):
         units = [(b, m) for b in range(B) for m in range(D_BLOCKS)]
         for unit in units[:AHEAD]:
             middle_tap(*unit)
+        grouped_tiles.append(regroup_rows(sources[-1][0]))
         right_tap(*units[0], 0)
         for i, unit in enumerate(units):
             if i + AHEAD < len(units):
@@ -202,6 +208,8 @@ def tile_cvim_pa_kernel(tc, x, w1, b1, w2, b2, out):
                 right_tap(*units[i + 1], 0)
             for n in range(CHUNKS):
                 left_tap(*unit, n)
+            if i == 0:
+                quantise(len(sources) - 1)
             if i > 0:
                 store_unit(*units[i - 1])
         store_unit(*units[-1])

from concourse import mybir
from concourse.masks import make_identity

F32 = mybir.dt.float32
BF16 = mybir.dt.bfloat16
U32 = mybir.dt.uint32
U8 = mybir.dt.uint8
FP8X4 = mybir.dt.float8_e4m3fn_x4
MULT = mybir.AluOpType.mult
ADD = mybir.AluOpType.add
SUBTRACT = mybir.AluOpType.subtract
IDENTITY = mybir.ActivationFunctionType.Identity

B, T, C, KW = 2, 1024, 512, 3
P = 128
PACK = 4
HALVES = 2
WORDS = C // 2
CHUNK = 512
ROW_BLOCKS = CHUNK // P
D_BLOCKS = C // P
CHUNKS = T // CHUNK
AHEAD = 2
WARM = 5

FLOPS = 2 * B * T * C * C + 2 * KW * B * T * C


def tile_cvim_pa_kernel(tc, x, w1, b1, w2, b2, out):
    nc = tc.nc

    with (
        tc.tile_pool(name="keep", bufs=1) as keep,
        tc.tile_pool(name="stage", bufs=3) as stage,
        tc.tile_pool(name="work", bufs=AHEAD + 3) as work,
        tc.tile_pool(name="leave", bufs=8) as leave,
        tc.psum_pool(name="psum", bufs=(AHEAD + 1) * CHUNKS) as psum,
        tc.psum_pool(name="psum_back", bufs=2) as psum_back,
        tc.manual_schedule(),
    ):
        zeros = keep.tile([P, CHUNK], BF16)
        nc.vector.memset(zeros[:], 0.0)
        unread = psum.tile([P, CHUNK], F32, tag="bank")
        for k in range(WARM):
            nc.tensor.matmul(out=unread[:], lhsT=zeros[:, 0:P], rhs=zeros[:], start=True, stop=True)

        taps_bf = keep.tile([P, D_BLOCKS, KW], BF16)
        b1_bf = keep.tile([P, D_BLOCKS], BF16)
        b2_bf = keep.tile([P, D_BLOCKS], BF16)
        with nc.allow_non_contiguous_dma(reason="one value of a 512-long vector to a partition"):
            nc.scalar.dma_start(out=taps_bf[:], in_=w2.rearrange("(m p) j -> p m j", p=P))
            nc.scalar.dma_start(out=b1_bf[:], in_=b1.rearrange("(m p) -> p m", p=P))
            nc.scalar.dma_start(out=b2_bf[:], in_=b2.rearrange("(m p) -> p m", p=P))

        def load_rows(rows_dram, name):
            rows = keep.tile([P, ROW_BLOCKS * C], BF16, name=name)
            for pair in range(ROW_BLOCKS // 2):
                nc.sync.dma_start(
                    out=rows[:, 2 * pair * C : (2 * pair + 2) * C].rearrange("p (r c) -> p r c", c=C),
                    in_=rows_dram[2 * pair * P : (2 * pair + 2) * P, :].rearrange("(r p) c -> p r c", p=P),
                )
            return rows

        w_rows = load_rows(w1, "w_rows")
        x_rows = {}
        for b in range(B):
            for n in range(CHUNKS):
                x_rows[b, n] = load_rows(x[b, n * CHUNK : (n + 1) * CHUNK, :], "x_rows_%d_%d" % (b, n))

        ident = keep.tile([P, P], F32)
        make_identity(nc, ident[:])

        taps = keep.tile([P, D_BLOCKS, KW], F32)
        nc.gpsimd.tensor_copy(out=taps[:], in_=taps_bf[:])
        tap_bias = keep.tile([P, D_BLOCKS, KW], F32)
        nc.gpsimd.tensor_tensor(
            out=tap_bias[:],
            in0=taps[:],
            in1=b1_bf[:].unsqueeze(2).to_broadcast([P, D_BLOCKS, KW]),
            op=MULT,
        )
        inner_bias = keep.tile([P, D_BLOCKS], F32)
        nc.gpsimd.tensor_tensor(out=inner_bias[:], in0=tap_bias[:, :, 0], in1=b2_bf[:], op=ADD)
        for j in range(1, KW):
            nc.gpsimd.tensor_tensor(out=inner_bias[:], in0=inner_bias[:], in1=tap_bias[:, :, j], op=ADD)

        def regroup_rows(rows):
            words = rows[:].bitcast(F32)
            grouped = stage.tile([P, CHUNK * PACK], BF16, align_bytes=64)
            grouped_words = grouped[:].bitcast(F32).rearrange("p (t u) -> p t u", u=HALVES)
            for pair in range(ROW_BLOCKS // 2):
                flipped = psum.tile([P, HALVES, 2 * P], F32, tag="bank")
                for r in (2 * pair, 2 * pair + 1):
                    for u in range(HALVES):
                        nc.tensor.transpose(
                            flipped[:, u, (r % 2) * P : (r % 2 + 1) * P],
                            words[:, r * WORDS + u * P : r * WORDS + (u + 1) * P],
                            ident[:],
                        )
                nc.scalar.copy(
                    out=grouped_words[:, 2 * pair * P : (2 * pair + 2) * P, :],
                    in_=flipped[:].rearrange("p u t -> p t u"),
                )
            return grouped

        w_codes = keep.tile([P, C], U32, align_bytes=64)
        w_scales = keep.tile([P, C], U8, align_bytes=64)
        x_codes = keep.tile([P, B, CHUNKS, CHUNK], U32, align_bytes=64)
        x_scales = keep.tile([P, B, CHUNKS, CHUNK], U8, align_bytes=64)
        sources = [(w_rows, w_codes[:], w_scales[:])]
        for b in range(B):
            for n in range(CHUNKS):
                sources.append((x_rows[b, n], x_codes[:, b, n, :], x_scales[:, b, n, :]))
        grouped_tiles = []

        def quantise(k):
            rows, codes, scales = sources[k]
            nc.vector.quantize_mx(out=codes.bitcast(FP8X4), scales=scales, in_=grouped_tiles[k][:])

        for k in range(len(sources) - 1):
            grouped_tiles.append(regroup_rows(sources[k][0]))
            quantise(k)

        acc = {}
        y_cols = {}

        def middle_tap(b, m):
            y = work.tile([P, T], F32, name="y_cols")
            y_cols[b, m] = y
            for n in range(CHUNKS):
                acc[b, m, n] = psum.tile([P, CHUNK], F32, name="acc", tag="bank")
                nc.tensor.matmul_mx(
                    out=acc[b, m, n][:],
                    lhsT=w_codes[:, m * P : (m + 1) * P].bitcast(FP8X4),
                    lhsT_scale=w_scales[:, m * P : (m + 1) * P],
                    rhs=x_codes[:, b, n, :].bitcast(FP8X4),
                    rhs_scale=x_scales[:, b, n, :],
                    start=True,
                    stop=True,
                )
            for n in range(CHUNKS):
                nc.scalar.activation(
                    out=y[:, n * CHUNK : (n + 1) * CHUNK],
                    in_=acc[b, m, n][:],
                    func=IDENTITY,
                    scale=taps[:, m, 1:2],
                    bias=inner_bias[:, m : m + 1],
                )
            nc.gpsimd.tensor_tensor(
                out=y[:, 0 : T : T - 1],
                in0=y[:, 0 : T : T - 1],
                in1=tap_bias[:, m, 0 : KW : KW - 1],
                op=SUBTRACT,
            )

        def right_tap(b, m, n):
            y = y_cols[b, m]
            t0 = n * CHUNK
            skip = 1 if n == 0 else 0
            nc.vector.scalar_tensor_tensor(
                out=y[:, t0 - 1 + skip : t0 + CHUNK - 1],
                in0=acc[b, m, n][:, skip:CHUNK],
                scalar=taps[:, m, 2:3],
                in1=y[:, t0 - 1 + skip : t0 + CHUNK - 1],
                op0=MULT,
                op1=ADD,
            )

        def left_tap(b, m, n):
            y = y_cols[b, m]
            t0 = n * CHUNK
            width = min(CHUNK, T - 1 - t0)
            nc.vector.scalar_tensor_tensor(
                out=y[:, t0 + 1 : t0 + 1 + width],
                in0=acc[b, m, n][:, 0:width],
                scalar=taps[:, m, 0:1],
                in1=y[:, t0 + 1 : t0 + 1 + width],
                op0=MULT,
                op1=ADD,
            )

        def store_unit(b, m):
            for n in range(CHUNKS):
                y_rows_ps = psum_back.tile([P, ROW_BLOCKS, P], F32)
                for k in range(ROW_BLOCKS):
                    t0 = n * CHUNK + k * P
                    nc.tensor.transpose(y_rows_ps[:, k, :], y_cols[b, m][:, t0 : t0 + P], ident[:])
                y_rows = leave.tile([P, ROW_BLOCKS, P], F32)
                nc.scalar.copy(out=y_rows[:], in_=y_rows_ps[:])
                nc.sync.dma_start(
                    out=out[b, n * CHUNK : (n + 1) * CHUNK, m * P : (m + 1) * P].rearrange(
                        "(k p) d -> p k d", p=P
                    ),
                    in_=y_rows[:],
                )

        units = [(b, m) for b in range(B) for m in range(D_BLOCKS)]
        for unit in units[:AHEAD]:
            middle_tap(*unit)
        grouped_tiles.append(regroup_rows(sources[-1][0]))
        right_tap(*units[0], 0)
        for i, unit in enumerate(units):
            if i + AHEAD < len(units):
                middle_tap(*units[i + AHEAD])
            for n in range(1, CHUNKS):
                right_tap(*unit, n)
            if i + 1 < len(units):
                right_tap(*units[i + 1], 0)
            for n in range(CHUNKS):
                left_tap(*unit, n)
            if i == 0:
                quantise(len(sources) - 1)
            if i > 0:
                store_unit(*units[i - 1])
        store_unit(*units[-1])
